import numpy as np
import ml_dtypes


def mxq(x, axis, fmt="e4m3"):
    dtype, down = {"e4m3": (ml_dtypes.float8_e4m3fn, 7), "e5m2": (ml_dtypes.float8_e5m2, 14)}[fmt]
    v = np.moveaxis(np.asarray(x, np.float32).astype(ml_dtypes.bfloat16).astype(np.float64), axis, -1)
    blocks = v.reshape(v.shape[:-1] + (-1, 32))
    amax = np.abs(blocks).max(-1, keepdims=True)
    byte = np.maximum(np.where(amax > 0, np.frexp(amax)[1] - 1 + 127, 0) - down, 1)
    scale = np.exp2(byte - 127.0)
    codes = (blocks / scale).astype(np.float32).astype(dtype).astype(np.float64)
    return np.moveaxis((codes * scale).reshape(v.shape), -1, axis)


WIDE = False


def mx_kscale(k):
    if not WIDE:
        return np.ones(k)
    levels = np.array([10, -10, 5, -5, 0])
    if k % 512:
        return np.exp2(np.random.permutation(np.resize(levels, k // 32))).repeat(32)
    a = np.empty((k // 512, 16))
    for p in range(k // 512):
        a[p, :8] = np.random.permutation(np.resize(levels, 8))
        for g in range(8):
            far = levels[np.abs(levels - a[p, g]) >= 10]
            a[p, g + 8] = far[np.random.randint(len(far))]
    return np.exp2(a.ravel()).repeat(32)


BF16 = ml_dtypes.bfloat16


def bf(x):
    return np.asarray(x, np.float32).astype(BF16)


def f64(x):
    return np.asarray(x).astype(np.float64)


B, C, H, W, DM, GH = 6, 1024, 16, 16, 128, 1024


def sigmoid(v):
    return 1.0 / (1.0 + np.exp(-v))


def setup_inputs():
    s = np.concatenate([mx_kscale(C), np.ones(C)])
    t = mx_kscale(GH)
    return {'x': bf(np.random.standard_normal((B, C, H, W)) * s[:C][None, :, None, None]),
            'agg': bf(np.random.standard_normal((B, C, H, W)) * 0.7),
            'g1w': bf(np.random.standard_normal((GH, 2 * C)) / np.sqrt(2 * C) * t[:, None] / s[None, :]),
            'g1b': bf(np.random.standard_normal(GH) * 0.3 * t),
            'g2w': bf(np.random.standard_normal((C, GH)) * 2.0 / np.sqrt(GH) / t[None, :]),
            'g2b': bf(np.random.standard_normal(C) * 0.3)}


def reference(x, agg, g1w, g1b, g2w, g2b):
    a = f64(agg).reshape(B, C, H * W)
    cat = np.concatenate([f64(x).reshape(B, C, H * W), a], axis=1)
    hidden = np.maximum((mxq(f64(g1w), 1, 'e4m3') @ mxq(cat, 1, 'e4m3')) + f64(g1b)[None, :, None], 0.0)
    gate = sigmoid((mxq(f64(g2w), 1, 'e4m3') @ mxq(hidden, 1, 'e4m3')) + f64(g2b)[None, :, None])
    return (a * gate).reshape(B, C, H, W)

@@ -1,0 +1,296 @@
+from contextlib import ExitStack
+
+import concourse.mybir as mybir
+from concourse.masks import make_identity
+
+F32 = mybir.dt.float32
+BF16 = mybir.dt.bfloat16
+U32 = mybir.dt.uint32
+U8 = mybir.dt.uint8
+FP8X4 = mybir.dt.float8_e4m3fn_x4
+ACT = mybir.ActivationFunctionType
+ALU = mybir.AluOpType
+
+P = 128
+PACK = 4
+HALVES = 2
+ROWS = 2
+QUARTERS = 4
+GROUPS = 2
+IMAGES = 6
+CH = 1024
+PIX = 256
+HID = 1024
+TILE_IMAGES = 2
+N_TILE = TILE_IMAGES * PIX
+N_TILES = IMAGES // TILE_IMAGES
+C_PASSES = 2 * CH // (P * PACK)
+X_PASSES = C_PASSES // 2
+G_PASSES = HID // (P * PACK)
+BANK_PASSES = 2
+PSUM_BANKS = 8
+RUN = 4
+
+FLOPS = 2 * IMAGES * PIX * (2 * CH * HID + HID * CH)
+
+
+def tile_graphaugmentation_pb_kernel(tc, x, agg, g1w, g1b, g2w, g2b, out):
+    nc = tc.nc
+
+    def by_quarters(images):
+        return images.rearrange("b (g p t) h w -> p b g t (h w)", g=GROUPS, p=P, t=PACK)
+
+    x_rows = by_quarters(x)
+    agg_rows = by_quarters(agg)
+    out_rows = by_quarters(out)
+    g1w_rows = g1w.rearrange("(g p t) c -> p g t c", g=GROUPS, p=P, t=PACK)
+    g2w_rows = g2w.rearrange("(g p t) k -> p g t k", g=GROUPS, p=P, t=PACK)
+
+    with ExitStack() as ctx:
+        keep = ctx.enter_context(tc.tile_pool(name="keep", bufs=1))
+        cat_stage = ctx.enter_context(tc.tile_pool(name="cat_stage", bufs=3))
+        w_stage = ctx.enter_context(tc.tile_pool(name="w_stage", bufs=4))
+        hid_stage = ctx.enter_context(tc.tile_pool(name="hid_stage", bufs=2))
+        res_stage = ctx.enter_context(tc.tile_pool(name="res_stage", bufs=5))
+        x_stage = ctx.enter_context(tc.tile_pool(name="x_stage", bufs=2))
+        psum = ctx.enter_context(tc.psum_pool(name="psum", bufs=PSUM_BANKS))
+        ctx.enter_context(tc.manual_schedule())
+
+        ident = keep.tile([P, P], F32, name="ident")
+        make_identity(nc, ident[:])
+
+        zero = keep.tile([P, 1], F32, name="zero")
+        half = keep.tile([P, 1], F32, name="half")
+        nc.vector.memset(zero[:], 0.0)
+        nc.scalar.activation(out=half[:], in_=zero[:], func=ACT.Sigmoid)
+
+        b1_bf = keep.tile([P, QUARTERS, ROWS], BF16, name="b1_bf")
+        b2_bf = keep.tile([P, QUARTERS, ROWS], BF16, name="b2_bf")
+
+        x_raw = []
+        agg_raw = [
+            keep.tile([P, TILE_IMAGES, QUARTERS * ROWS, PIX], BF16, name="agg_raw%d" % j)
+            for j in range(N_TILES)
+        ]
+        w1_raw = [keep.tile([P, ROWS, 2 * CH], BF16, name="w1_raw%d" % v) for v in range(QUARTERS)]
+        w2_raw = [keep.tile([P, ROWS, HID], BF16, name="w2_raw%d" % v) for v in range(QUARTERS)]
+
+        def load_cat(j):
+            x_raw.append(x_stage.tile([P, TILE_IMAGES, QUARTERS * ROWS, PIX], BF16, name="x_raw"))
+            for raw, rows in ((x_raw[j], x_rows), (agg_raw[j], agg_rows)):
+                for b in range(TILE_IMAGES):
+                    nc.sync.dma_start(
+                        out=raw[:, b].rearrange("p (g t) w -> p g t w", t=PACK),
+                        in_=rows[:, TILE_IMAGES * j + b],
+                    )
+
+        first_quarters = QUARTERS // 2
+        load_cat(0)
+        for v in range(QUARTERS):
+            if v == first_quarters:
+                for b_bf, b_dram in ((b1_bf, g1b), (b2_bf, g2b)):
+                    nc.sync.dma_start(
+                        out=b_bf[:].rearrange("p (g h) e -> p g (h e)", g=GROUPS),
+                        in_=b_dram.rearrange("(g p t) -> p g t", g=GROUPS, p=P, t=PACK),
+                    )
+            for e in range(ROWS):
+                nc.sync.dma_start(out=w1_raw[v][:, e], in_=g1w_rows[:, v // HALVES, ROWS * (v % HALVES) + e])
+        load_cat(1)
+        for v in range(QUARTERS):
+            pair = ROWS * (v % HALVES)
+            nc.sync.dma_start(out=w2_raw[v][:], in_=g2w_rows[:, v // HALVES, pair : pair + ROWS])
+
+        b1 = keep.tile([P, QUARTERS, ROWS], F32, name="b1")
+        b2 = keep.tile([P, QUARTERS, ROWS], F32, name="b2")
+
+        cat_codes = [
+            keep.tile([P, C_PASSES, N_TILE], U32, name="cat_codes%d" % j, align_bytes=64)
+            for j in range(N_TILES)
+        ]
+        cat_scales = [
+            keep.tile([P, C_PASSES, N_TILE], U8, name="cat_scales%d" % j, align_bytes=64)
+            for j in range(N_TILES)
+        ]
+        hid_codes = [
+            keep.tile([P, G_PASSES, N_TILE], U32, name="hid_codes%d" % j, align_bytes=64)
+            for j in range(N_TILES)
+        ]
+        hid_scales = [
+            keep.tile([P, G_PASSES, N_TILE], U8, name="hid_scales%d" % j, align_bytes=64)
+            for j in range(N_TILES)
+        ]
+        w1_codes = [
+            keep.tile([P, ROWS, C_PASSES, P], U32, name="w1_codes%d" % v, align_bytes=64)
+            for v in range(QUARTERS)
+        ]
+        w1_scales = [
+            keep.tile([P, ROWS, C_PASSES, P], U8, name="w1_scales%d" % v, align_bytes=64)
+            for v in range(QUARTERS)
+        ]
+        w2_codes = [
+            keep.tile([P, ROWS, G_PASSES, P], U32, name="w2_codes%d" % v, align_bytes=64)
+            for v in range(QUARTERS)
+        ]
+        w2_scales = [
+            keep.tile([P, ROWS, G_PASSES, P], U8, name="w2_scales%d" % v, align_bytes=64)
+            for v in range(QUARTERS)
+        ]
+
+        def prepare_cat_half(j, x_half):
+            raw = x_raw[j] if x_half else agg_raw[j]
+            passes = (0, 1) if x_half else (3, 2)
+            tiles = []
+            for G in passes:
+                first = PACK * (G % X_PASSES)
+                grouped = cat_stage.tile([P, N_TILE, PACK], BF16, name="cat_grouped", align_bytes=64)
+                dst = grouped[:].rearrange("p (b c i) t -> p b c t i", b=TILE_IMAGES, i=RUN)
+                src = raw[:, :, first : first + PACK, :].rearrange("p b t (c i) -> p b c t i", i=RUN)
+                if G == C_PASSES - 1:
+                    for b in range(TILE_IMAGES):
+                        nc.scalar.copy(out=dst[:, b], in_=src[:, b])
+                else:
+                    nc.vector.tensor_copy(out=dst, in_=src)
+                tiles.append(grouped)
+            for G, grouped in zip(passes, tiles):
+                nc.vector.quantize_mx(
+                    out=cat_codes[j][:, G, :].bitcast(FP8X4),
+                    scales=cat_scales[j][:, G, :],
+                    in_=grouped[:].rearrange("p n t -> p (n t)"),
+                )
+
+        def prepare_weights(raw, rows, passes, codes, scales):
+            words = raw[:].bitcast(F32)
+            grouped = w_stage.tile([P, len(rows), passes, P, PACK], BF16, name="w_grouped", align_bytes=64)
+            grouped_words = grouped[:].bitcast(F32)
+            for i, e in enumerate(rows):
+                for G0 in range(0, passes, BANK_PASSES):
+                    bank = psum.tile([P, BANK_PASSES, HALVES, P], F32, name="t_bank", tag="bank")
+                    for G in range(G0, G0 + BANK_PASSES):
+                        for u in range(HALVES):
+                            first = P * HALVES * G
+                            nc.tensor.transpose(
+                                out=bank[:, G - G0, u, :],
+                                in_=words[:, e, first + u : first + P * HALVES : HALVES],
+                                identity=ident[:],
+                            )
+                    nc.scalar.copy(
+                        out=grouped_words[:, i, G0 : G0 + BANK_PASSES, :, :],
+                        in_=bank[:].rearrange("p g u m -> p g m u"),
+                    )
+            these = slice(rows[0], rows[0] + len(rows))
+            nc.vector.quantize_mx(
+                out=codes[:, these].rearrange("p e g m -> p (e g m)").bitcast(FP8X4),
+                scales=scales[:, these].rearrange("p e g m -> p (e g m)"),
+                in_=grouped[:].rearrange("p e g m t -> p (e g m t)"),
+            )
+
+        def prepare_w1(v):
+            for e in range(ROWS):
+                prepare_weights(w1_raw[v], (e,), C_PASSES, w1_codes[v], w1_scales[v])
+
+        def prepare_w2(v):
+            prepare_weights(w2_raw[v], (0, 1), G_PASSES, w2_codes[v], w2_scales[v])
+
+        def product(w_codes, w_scales, e, passes, rhs_codes, rhs_scales):
+            acc = psum.tile([P, N_TILE], F32, name="acc", tag="bank")
+            for G in range(passes):
+                nc.tensor.matmul_mx(
+                    out=acc[:],
+                    lhsT=w_codes[:, e, G, :].bitcast(FP8X4),
+                    lhsT_scale=w_scales[:, e, G, :],
+                    rhs=rhs_codes[:, G, :].bitcast(FP8X4),
+                    rhs_scale=rhs_scales[:, G, :],
+                    start=(G == 0),
+                    stop=(G == passes - 1),
+                )
+            return acc
+
+        def new_hid():
+            return hid_stage.tile([P, PACK, N_TILE], BF16, name="hid")
+
+        def hidden_unit(j, v, e, hid):
+            acc = product(w1_codes[v], w1_scales[v], e, C_PASSES, cat_codes[j], cat_scales[j])
+            nc.scalar.activation(
+                out=hid[:, ROWS * (v % HALVES) + e, :],
+                in_=acc[:],
+                func=ACT.Relu,
+                bias=b1[:, v, e : e + 1],
+                scale=1.0,
+            )
+
+        def quantise_hidden(j, G, hid):
+            grouped = hid_stage.tile([P, N_TILE, PACK], BF16, name="hid_grouped", align_bytes=64)
+            nc.vector.tensor_copy(
+                out=grouped[:].rearrange("p (c i) t -> p c t i", i=RUN),
+                in_=hid[:].rearrange("p t (c i) -> p c t i", i=RUN),
+            )
+            nc.vector.quantize_mx(
+                out=hid_codes[j][:, G, :].bitcast(FP8X4),
+                scales=hid_scales[j][:, G, :],
+                in_=grouped[:].rearrange("p n t -> p (n t)"),
+            )
+
+        def gate_products(j, v):
+            res = res_stage.tile([P, TILE_IMAGES, ROWS, PIX], F32, name="res")
+            for e in range(ROWS):
+                acc = product(w2_codes[v], w2_scales[v], e, G_PASSES, hid_codes[j], hid_scales[j])
+                nc.scalar.activation(
+                    out=res[:, :, e, :],
+                    in_=acc[:].rearrange("p (b w) -> p b w", b=TILE_IMAGES),
+                    func=ACT.Sigmoid,
+                    bias=b2[:, v, e : e + 1],
+                    scale=1.0,
+                )
+            return res
+
+        def gate_apply(j, v, res):
+            nc.vector.tensor_tensor(
+                out=res[:], in0=res[:], in1=agg_raw[j][:, :, ROWS * v : ROWS * v + ROWS, :], op=ALU.mult
+            )
+            pair = ROWS * (v % HALVES)
+            nc.sync.dma_start(
+                out=out_rows[:, TILE_IMAGES * j : TILE_IMAGES * j + TILE_IMAGES, v // HALVES, pair : pair + ROWS],
+                in_=res[:],
+            )
+
+        prepare_cat_half(0, True)
+        prepare_cat_half(0, False)
+        load_cat(2)
+        for v in range(first_quarters):
+            prepare_w1(v)
+        nc.vector.tensor_copy(out=b1[:], in_=b1_bf[:])
+        nc.vector.tensor_copy(out=b2[:], in_=b2_bf[:])
+
+        for v in range(QUARTERS):
+            if v % HALVES == 0:
+                hid = new_hid()
+            for e in range(ROWS):
+                hidden_unit(0, v, e, hid)
+                if v == 0:
+                    prepare_w1(first_quarters + e)
+            if v < 2:
+                prepare_cat_half(1, v == 0)
+            if v == 1:
+                quantise_hidden(0, 0, hid)
+        prepare_w2(0)
+        quantise_hidden(0, 1, hid)
+        for v in range(1, QUARTERS):
+            prepare_w2(v)
+
+        for j in range(1, N_TILES):
+            for v in range(QUARTERS):
+                if v % HALVES == 0:
+                    hid = new_hid()
+                for e in range(ROWS):
+                    hidden_unit(j, v, e, hid)
+                if v > 0:
+                    res = gate_products(j - 1, v - 1)
+                if j + 1 < N_TILES and v < 2:
+                    prepare_cat_half(j + 1, v == 0)
+                if v % HALVES == 1:
+                    quantise_hidden(j, v // HALVES, hid)
+                if v > 0:
+                    gate_apply(j - 1, v - 1, res)
+            gate_apply(j - 1, QUARTERS - 1, gate_products(j - 1, QUARTERS - 1))
+        for v in range(QUARTERS):
+            gate_apply(N_TILES - 1, v, gate_products(N_TILES - 1, v))

@@ -13,17 +13,13 @@ ALU = mybir.AluOpType
 
 P = 128
 PACK = 4
-HALVES = 2
-ROWS = 2
-QUARTERS = 4
 GROUPS = 2
+UNITS = GROUPS * PACK
+HALVES = 2
 IMAGES = 6
 CH = 1024
 PIX = 256
 HID = 1024
-TILE_IMAGES = 2
-N_TILE = TILE_IMAGES * PIX
-N_TILES = IMAGES // TILE_IMAGES
 C_PASSES = 2 * CH // (P * PACK)
 X_PASSES = C_PASSES // 2
 G_PASSES = HID // (P * PACK)
@@ -31,27 +27,30 @@ BANK_PASSES = 2
 PSUM_BANKS = 8
 RUN = 4
 
+TILES = ((0,), (1,), (2, 3), (4,), (5,))
+
 FLOPS = 2 * IMAGES * PIX * (2 * CH * HID + HID * CH)
 
 
 def tile_graphaugmentation_pb_kernel(tc, x, agg, g1w, g1b, g2w, g2b, out):
     nc = tc.nc
 
-    def by_quarters(images):
+    def by_units(images):
         return images.rearrange("b (g p t) h w -> p b g t (h w)", g=GROUPS, p=P, t=PACK)
 
-    x_rows = by_quarters(x)
-    agg_rows = by_quarters(agg)
-    out_rows = by_quarters(out)
+    x_rows = by_units(x)
+    agg_rows = by_units(agg)
+    out_rows = by_units(out)
     g1w_rows = g1w.rearrange("(g p t) c -> p g t c", g=GROUPS, p=P, t=PACK)
     g2w_rows = g2w.rearrange("(g p t) k -> p g t k", g=GROUPS, p=P, t=PACK)
 
     with ExitStack() as ctx:
         keep = ctx.enter_context(tc.tile_pool(name="keep", bufs=1))
-        cat_stage = ctx.enter_context(tc.tile_pool(name="cat_stage", bufs=3))
+        cat_stage = ctx.enter_context(tc.tile_pool(name="cat_stage", bufs=4))
         w_stage = ctx.enter_context(tc.tile_pool(name="w_stage", bufs=4))
+        w_raw_stage = ctx.enter_context(tc.tile_pool(name="w_raw_stage", bufs=UNITS))
         hid_stage = ctx.enter_context(tc.tile_pool(name="hid_stage", bufs=2))
-        res_stage = ctx.enter_context(tc.tile_pool(name="res_stage", bufs=5))
+        res_stage = ctx.enter_context(tc.tile_pool(name="res_stage", bufs=8))
         x_stage = ctx.enter_context(tc.tile_pool(name="x_stage", bufs=2))
         psum = ctx.enter_context(tc.psum_pool(name="psum", bufs=PSUM_BANKS))
         ctx.enter_context(tc.manual_schedule())
@@ -64,140 +63,146 @@ def tile_graphaugmentation_pb_kernel(tc, x, agg, g1w, g1b, g2w, g2b, out):
         nc.vector.memset(zero[:], 0.0)
         nc.scalar.activation(out=half[:], in_=zero[:], func=ACT.Sigmoid)
 
-        b1_bf = keep.tile([P, QUARTERS, ROWS], BF16, name="b1_bf")
-        b2_bf = keep.tile([P, QUARTERS, ROWS], BF16, name="b2_bf")
+        b1 = keep.tile([P, UNITS], BF16, name="b1")
+        b2 = keep.tile([P, UNITS], BF16, name="b2")
 
-        x_raw = []
-        agg_raw = [
-            keep.tile([P, TILE_IMAGES, QUARTERS * ROWS, PIX], BF16, name="agg_raw%d" % j)
-            for j in range(N_TILES)
-        ]
-        w1_raw = [keep.tile([P, ROWS, 2 * CH], BF16, name="w1_raw%d" % v) for v in range(QUARTERS)]
-        w2_raw = [keep.tile([P, ROWS, HID], BF16, name="w2_raw%d" % v) for v in range(QUARTERS)]
+        def load_rows(raw, rows, images):
+            for n, b in enumerate(images):
+                nc.sync.dma_start(out=raw[:, n].rearrange("p (g t) w -> p g t w", t=PACK), in_=rows[:, b])
 
-        def load_cat(j):
-            x_raw.append(x_stage.tile([P, TILE_IMAGES, QUARTERS * ROWS, PIX], BF16, name="x_raw"))
-            for raw, rows in ((x_raw[j], x_rows), (agg_raw[j], agg_rows)):
-                for b in range(TILE_IMAGES):
-                    nc.sync.dma_start(
-                        out=raw[:, b].rearrange("p (g t) w -> p g t w", t=PACK),
-                        in_=rows[:, TILE_IMAGES * j + b],
-                    )
+        def load_x(j):
+            pool = x_stage if len(TILES[j]) == 1 else keep
+            raw = pool.tile([P, len(TILES[j]), UNITS, PIX], BF16, name="x_raw%d" % len(TILES[j]))
+            load_rows(raw, x_rows, TILES[j])
+            return raw
 
-        first_quarters = QUARTERS // 2
-        load_cat(0)
-        for v in range(QUARTERS):
-            if v == first_quarters:
-                for b_bf, b_dram in ((b1_bf, g1b), (b2_bf, g2b)):
-                    nc.sync.dma_start(
-                        out=b_bf[:].rearrange("p (g h) e -> p g (h e)", g=GROUPS),
-                        in_=b_dram.rearrange("(g p t) -> p g t", g=GROUPS, p=P, t=PACK),
-                    )
-            for e in range(ROWS):
-                nc.sync.dma_start(out=w1_raw[v][:, e], in_=g1w_rows[:, v // HALVES, ROWS * (v % HALVES) + e])
-        load_cat(1)
-        for v in range(QUARTERS):
-            pair = ROWS * (v % HALVES)
-            nc.sync.dma_start(out=w2_raw[v][:], in_=g2w_rows[:, v // HALVES, pair : pair + ROWS])
+        def load_agg(j):
+            raw = keep.tile([P, len(TILES[j]), UNITS, PIX], BF16, name="agg_raw%d" % j)
+            load_rows(raw, agg_rows, TILES[j])
+            return raw
 
-        b1 = keep.tile([P, QUARTERS, ROWS], F32, name="b1")
-        b2 = keep.tile([P, QUARTERS, ROWS], F32, name="b2")
+        def load_w1(i):
+            raw = w_raw_stage.tile([P, 2 * CH], BF16, name="w_raw")
+            nc.sync.dma_start(out=raw[:], in_=g1w_rows[:, i // PACK, i % PACK])
+            return raw
 
-        cat_codes = [
-            keep.tile([P, C_PASSES, N_TILE], U32, name="cat_codes%d" % j, align_bytes=64)
-            for j in range(N_TILES)
-        ]
-        cat_scales = [
-            keep.tile([P, C_PASSES, N_TILE], U8, name="cat_scales%d" % j, align_bytes=64)
-            for j in range(N_TILES)
-        ]
-        hid_codes = [
-            keep.tile([P, G_PASSES, N_TILE], U32, name="hid_codes%d" % j, align_bytes=64)
-            for j in range(N_TILES)
-        ]
-        hid_scales = [
-            keep.tile([P, G_PASSES, N_TILE], U8, name="hid_scales%d" % j, align_bytes=64)
-            for j in range(N_TILES)
-        ]
-        w1_codes = [
-            keep.tile([P, ROWS, C_PASSES, P], U32, name="w1_codes%d" % v, align_bytes=64)
-            for v in range(QUARTERS)
-        ]
-        w1_scales = [
-            keep.tile([P, ROWS, C_PASSES, P], U8, name="w1_scales%d" % v, align_bytes=64)
-            for v in range(QUARTERS)
-        ]
-        w2_codes = [
-            keep.tile([P, ROWS, G_PASSES, P], U32, name="w2_codes%d" % v, align_bytes=64)
-            for v in range(QUARTERS)
-        ]
-        w2_scales = [
-            keep.tile([P, ROWS, G_PASSES, P], U8, name="w2_scales%d" % v, align_bytes=64)
-            for v in range(QUARTERS)
-        ]
+        def load_w2(i):
+            raw = w_raw_stage.tile([P, 2, HID], BF16, name="w_raw")
+            nc.sync.dma_start(out=raw[:], in_=g2w_rows[:, i // PACK, i % PACK : i % PACK + 2])
+            return raw
 
-        def prepare_cat_half(j, x_half):
-            raw = x_raw[j] if x_half else agg_raw[j]
-            passes = (0, 1) if x_half else (3, 2)
-            tiles = []
-            for G in passes:
-                first = PACK * (G % X_PASSES)
-                grouped = cat_stage.tile([P, N_TILE, PACK], BF16, name="cat_grouped", align_bytes=64)
-                dst = grouped[:].rearrange("p (b c i) t -> p b c t i", b=TILE_IMAGES, i=RUN)
-                src = raw[:, :, first : first + PACK, :].rearrange("p b t (c i) -> p b c t i", i=RUN)
-                if G == C_PASSES - 1:
-                    for b in range(TILE_IMAGES):
-                        nc.scalar.copy(out=dst[:, b], in_=src[:, b])
-                else:
-                    nc.vector.tensor_copy(out=dst, in_=src)
-                tiles.append(grouped)
-            for G, grouped in zip(passes, tiles):
-                nc.vector.quantize_mx(
-                    out=cat_codes[j][:, G, :].bitcast(FP8X4),
-                    scales=cat_scales[j][:, G, :],
-                    in_=grouped[:].rearrange("p n t -> p (n t)"),
-                )
+        x_raw = {}
+        agg_raw = {}
+        w1_raw = {}
+        w2_raw = {}
+        w1_raw[0] = load_w1(0)
+        x_raw[0] = load_x(0)
+        w1_raw[1] = load_w1(1)
+        agg_raw[0] = load_agg(0)
+        w1_raw[2] = load_w1(2)
+        w1_raw[3] = load_w1(3)
+        for b_bf, b_dram in ((b1, g1b), (b2, g2b)):
+            nc.sync.dma_start(
+                out=b_bf[:].rearrange("p (g t) -> p g t", g=GROUPS),
+                in_=b_dram.rearrange("(g p t) -> p g t", g=GROUPS, p=P, t=PACK),
+            )
+        x_raw[1] = load_x(1)
+        agg_raw[1] = load_agg(1)
+        for i in range(4, UNITS):
+            w1_raw[i] = load_w1(i)
 
-        def prepare_weights(raw, rows, passes, codes, scales):
-            words = raw[:].bitcast(F32)
-            grouped = w_stage.tile([P, len(rows), passes, P, PACK], BF16, name="w_grouped", align_bytes=64)
-            grouped_words = grouped[:].bitcast(F32)
-            for i, e in enumerate(rows):
-                for G0 in range(0, passes, BANK_PASSES):
-                    bank = psum.tile([P, BANK_PASSES, HALVES, P], F32, name="t_bank", tag="bank")
-                    for G in range(G0, G0 + BANK_PASSES):
-                        for u in range(HALVES):
-                            first = P * HALVES * G
-                            nc.tensor.transpose(
-                                out=bank[:, G - G0, u, :],
-                                in_=words[:, e, first + u : first + P * HALVES : HALVES],
-                                identity=ident[:],
-                            )
-                    nc.scalar.copy(
-                        out=grouped_words[:, i, G0 : G0 + BANK_PASSES, :, :],
-                        in_=bank[:].rearrange("p g u m -> p g m u"),
-                    )
-            these = slice(rows[0], rows[0] + len(rows))
+        def operand(name, shape):
+            codes = keep.tile([P] + shape, U32, name=name + "_codes", align_bytes=64)
+            scales = keep.tile([P] + shape, U8, name=name + "_scales", align_bytes=64)
+            return codes, scales
+
+        cat_mx = [operand("cat%d" % j, [C_PASSES, PIX * len(TILES[j])]) for j in range(len(TILES))]
+        hid_mx = [operand("hid%d" % j, [G_PASSES, PIX * len(TILES[j])]) for j in range(len(TILES))]
+        w1_mx = [operand("w1_%d" % i, [C_PASSES, P]) for i in range(UNITS)]
+        w2_mx = [operand("w2_%d" % i, [2, G_PASSES, P]) for i in range(0, UNITS, 2)]
+
+        def quantise(mx, where, grouped):
+            codes, scales = mx
             nc.vector.quantize_mx(
-                out=codes[:, these].rearrange("p e g m -> p (e g m)").bitcast(FP8X4),
-                scales=scales[:, these].rearrange("p e g m -> p (e g m)"),
-                in_=grouped[:].rearrange("p e g m t -> p (e g m t)"),
+                out=codes[:, where].rearrange("p a n -> p (a n)").bitcast(FP8X4),
+                scales=scales[:, where].rearrange("p a n -> p (a n)"),
+                in_=grouped,
             )
 
-        def prepare_w1(v):
-            for e in range(ROWS):
-                prepare_weights(w1_raw[v], (e,), C_PASSES, w1_codes[v], w1_scales[v])
+        def regroup_image(raw, shared):
+            grouped = cat_stage.tile([P, X_PASSES, PIX, PACK], BF16, name="cat_grouped", align_bytes=64)
+            dst = grouped[:].rearrange("p g (c i) t -> p g c t i", i=RUN)
+            src = raw[:, 0].rearrange("p (g t) (c i) -> p g c t i", t=PACK, i=RUN)
+            if shared:
+                nc.vector.tensor_copy(out=dst[:, 0], in_=src[:, 0])
+                nc.scalar.copy(out=dst[:, 1], in_=src[:, 1])
+            else:
+                nc.vector.tensor_copy(out=dst, in_=src)
+            return grouped
 
-        def prepare_w2(v):
-            prepare_weights(w2_raw[v], (0, 1), G_PASSES, w2_codes[v], w2_scales[v])
+        def quantise_image(j, first, grouped):
+            quantise(cat_mx[j], slice(first, first + X_PASSES), grouped[:].rearrange("p g n t -> p (g n t)"))
 
-        def product(w_codes, w_scales, e, passes, rhs_codes, rhs_scales):
-            acc = psum.tile([P, N_TILE], F32, name="acc", tag="bank")
+        def regroup_pass(raw, g, engine_copy):
+            grouped = cat_stage.tile([P, 2, PIX, PACK], BF16, name="cat_grouped", align_bytes=64)
+            dst = grouped[:].rearrange("p b (c i) t -> p b c t i", i=RUN)
+            src = raw[:, :, PACK * g : PACK * g + PACK, :].rearrange("p b t (c i) -> p b c t i", i=RUN)
+            if engine_copy == "scalar":
+                for b in range(2):
+                    nc.scalar.copy(out=dst[:, b], in_=src[:, b])
+            else:
+                nc.vector.tensor_copy(out=dst, in_=src)
+            return grouped
+
+        def quantise_pass(j, G, grouped):
+            quantise(cat_mx[j], slice(G, G + 1), grouped[:].rearrange("p b n t -> p (b n t)"))
+
+        def transpose_rows(words, passes, grouped_words):
+            for G0 in range(0, passes, BANK_PASSES):
+                bank = psum.tile([P, BANK_PASSES, HALVES, P], F32, name="t_bank", tag="bank")
+                for G in range(G0, G0 + BANK_PASSES):
+                    for u in range(HALVES):
+                        first = P * HALVES * G
+                        nc.tensor.transpose(
+                            out=bank[:, G - G0, u, :],
+                            in_=words[:, first + u : first + P * HALVES : HALVES],
+                            identity=ident[:],
+                        )
+                nc.scalar.copy(
+                    out=grouped_words[:, G0 : G0 + BANK_PASSES, :, :],
+                    in_=bank[:].rearrange("p g u m -> p g m u"),
+                )
+
+        w_grouped = {}
+
+        def transpose_w1(i):
+            w_grouped[i] = w_stage.tile([P, C_PASSES, P, PACK], BF16, name="w_grouped", align_bytes=64)
+            transpose_rows(w1_raw[i][:].bitcast(F32), C_PASSES, w_grouped[i][:].bitcast(F32))
+
+        def quantise_w1(i):
+            quantise(w1_mx[i], slice(0, C_PASSES), w_grouped[i][:].rearrange("p g m t -> p (g m t)"))
+
+        def transpose_w2(i):
+            w_grouped[i] = w_stage.tile([P, 2, G_PASSES, P, PACK], BF16, name="w_grouped", align_bytes=64)
+            for e in range(2):
+                transpose_rows(w2_raw[i][:].bitcast(F32)[:, e], G_PASSES, w_grouped[i][:].bitcast(F32)[:, e])
+
+        def quantise_w2(i):
+            codes, scales = w2_mx[i // 2]
+            nc.vector.quantize_mx(
+                out=codes[:].rearrange("p e g m -> p (e g m)").bitcast(FP8X4),
+                scales=scales[:].rearrange("p e g m -> p (e g m)"),
+                in_=w_grouped[i][:].rearrange("p e g m t -> p (e g m t)"),
+            )
+
+        def product(codes, scales, passes, rhs):
+            rhs_codes, rhs_scales = rhs
+            acc = psum.tile([P, rhs_codes.shape[2]], F32, name="acc", tag="bank")
             for G in range(passes):
                 nc.tensor.matmul_mx(
                     out=acc[:],
-                    lhsT=w_codes[:, e, G, :].bitcast(FP8X4),
-                    lhsT_scale=w_scales[:, e, G, :],
+                    lhsT=codes[:, G, :].bitcast(FP8X4),
+                    lhsT_scale=scales[:, G, :],
                     rhs=rhs_codes[:, G, :].bitcast(FP8X4),
                     rhs_scale=rhs_scales[:, G, :],
                     start=(G == 0),
@@ -205,92 +210,170 @@ def tile_graphaugmentation_pb_kernel(tc, x, agg, g1w, g1b, g2w, g2b, out):
                 )
             return acc
 
-        def new_hid():
-            return hid_stage.tile([P, PACK, N_TILE], BF16, name="hid")
+        hid = {}
 
-        def hidden_unit(j, v, e, hid):
-            acc = product(w1_codes[v], w1_scales[v], e, C_PASSES, cat_codes[j], cat_scales[j])
-            nc.scalar.activation(
-                out=hid[:, ROWS * (v % HALVES) + e, :],
-                in_=acc[:],
-                func=ACT.Relu,
-                bias=b1[:, v, e : e + 1],
-                scale=1.0,
-            )
-
-        def quantise_hidden(j, G, hid):
-            grouped = hid_stage.tile([P, N_TILE, PACK], BF16, name="hid_grouped", align_bytes=64)
-            nc.vector.tensor_copy(
-                out=grouped[:].rearrange("p (c i) t -> p c t i", i=RUN),
-                in_=hid[:].rearrange("p t (c i) -> p c t i", i=RUN),
-            )
-            nc.vector.quantize_mx(
-                out=hid_codes[j][:, G, :].bitcast(FP8X4),
-                scales=hid_scales[j][:, G, :],
-                in_=grouped[:].rearrange("p n t -> p (n t)"),
-            )
-
-        def gate_products(j, v):
-            res = res_stage.tile([P, TILE_IMAGES, ROWS, PIX], F32, name="res")
-            for e in range(ROWS):
-                acc = product(w2_codes[v], w2_scales[v], e, G_PASSES, hid_codes[j], hid_scales[j])
+        def hidden(j, units):
+            for i in units:
+                G = i // PACK
+                if i % PACK == 0:
+                    hid[j, G] = hid_stage.tile([P, PACK, PIX * len(TILES[j])], BF16, name="hid%d" % len(TILES[j]))
+                acc = product(w1_mx[i][0], w1_mx[i][1], C_PASSES, cat_mx[j])
                 nc.scalar.activation(
-                    out=res[:, :, e, :],
-                    in_=acc[:].rearrange("p (b w) -> p b w", b=TILE_IMAGES),
+                    out=hid[j, G][:, i % PACK, :], in_=acc[:], func=ACT.Relu, bias=b1[:, i : i + 1], scale=1.0
+                )
+
+        hid_grouped = {}
+
+        def regroup_hidden(j, G):
+            columns = PIX * len(TILES[j])
+            hid_grouped[j, G] = hid_stage.tile(
+                [P, columns, PACK], BF16, name="hid_grouped%d" % len(TILES[j]), align_bytes=64
+            )
+            nc.vector.tensor_copy(
+                out=hid_grouped[j, G][:].rearrange("p (c i) t -> p c t i", i=RUN),
+                in_=hid[j, G][:].rearrange("p t (c i) -> p c t i", i=RUN),
+            )
+
+        def quantise_hidden(j, G):
+            quantise(hid_mx[j], slice(G, G + 1), hid_grouped[j, G][:].rearrange("p n t -> p (n t)"))
+
+        def gate(j, units):
+            images = len(TILES[j])
+            res = res_stage.tile([P, images, len(units), PIX], F32, name="res")
+            for n, i in enumerate(units):
+                codes, scales = w2_mx[i // 2]
+                acc = product(codes[:, i % 2], scales[:, i % 2], G_PASSES, hid_mx[j])
+                nc.scalar.activation(
+                    out=res[:, :, n, :],
+                    in_=acc[:].rearrange("p (b w) -> p b w", b=images),
                     func=ACT.Sigmoid,
-                    bias=b2[:, v, e : e + 1],
+                    bias=b2[:, i : i + 1],
                     scale=1.0,
                 )
             return res
 
-        def gate_apply(j, v, res):
+        def apply_gate(j, units, res):
+            first, last = units[0], units[-1]
             nc.vector.tensor_tensor(
-                out=res[:], in0=res[:], in1=agg_raw[j][:, :, ROWS * v : ROWS * v + ROWS, :], op=ALU.mult
+                out=res[:], in0=res[:], in1=agg_raw[j][:, :, first : last + 1, :], op=ALU.mult
             )
-            pair = ROWS * (v % HALVES)
+            b0 = TILES[j][0]
+            t0 = first % PACK
             nc.sync.dma_start(
-                out=out_rows[:, TILE_IMAGES * j : TILE_IMAGES * j + TILE_IMAGES, v // HALVES, pair : pair + ROWS],
-                in_=res[:],
+                out=out_rows[:, b0 : b0 + len(TILES[j]), first // PACK, t0 : t0 + len(units)], in_=res[:]
             )
 
-        prepare_cat_half(0, True)
-        prepare_cat_half(0, False)
-        load_cat(2)
-        for v in range(first_quarters):
-            prepare_w1(v)
-        nc.vector.tensor_copy(out=b1[:], in_=b1_bf[:])
-        nc.vector.tensor_copy(out=b2[:], in_=b2_bf[:])
-
-        for v in range(QUARTERS):
-            if v % HALVES == 0:
-                hid = new_hid()
-            for e in range(ROWS):
-                hidden_unit(0, v, e, hid)
-                if v == 0:
-                    prepare_w1(first_quarters + e)
-            if v < 2:
-                prepare_cat_half(1, v == 0)
-            if v == 1:
-                quantise_hidden(0, 0, hid)
-        prepare_w2(0)
-        quantise_hidden(0, 1, hid)
-        for v in range(1, QUARTERS):
-            prepare_w2(v)
-
-        for j in range(1, N_TILES):
-            for v in range(QUARTERS):
-                if v % HALVES == 0:
-                    hid = new_hid()
-                for e in range(ROWS):
-                    hidden_unit(j, v, e, hid)
-                if v > 0:
-                    res = gate_products(j - 1, v - 1)
-                if j + 1 < N_TILES and v < 2:
-                    prepare_cat_half(j + 1, v == 0)
-                if v % HALVES == 1:
-                    quantise_hidden(j, v // HALVES, hid)
-                if v > 0:
-                    gate_apply(j - 1, v - 1, res)
-            gate_apply(j - 1, QUARTERS - 1, gate_products(j - 1, QUARTERS - 1))
-        for v in range(QUARTERS):
-            gate_apply(N_TILES - 1, v, gate_products(N_TILES - 1, v))
+        low, high = (0, 1, 2, 3), (4, 5, 6, 7)
+        transpose_w1(0)
+        x0 = regroup_image(x_raw[0], False)
+        quantise_w1(0)
+        quantise_image(0, 0, x0)
+        transpose_w1(1)
+        a0 = regroup_image(agg_raw[0], False)
+        quantise_w1(1)
+        quantise_image(0, X_PASSES, a0)
+        transpose_w1(2)
+        transpose_w1(3)
+        hidden(0, (0, 1))
+        quantise_w1(2)
+        quantise_w1(3)
+        x1 = regroup_image(x_raw[1], False)
+        x_raw[2] = load_x(2)
+        w2_raw[0] = load_w2(0)
+        w2_raw[2] = load_w2(2)
+        agg_raw[2] = load_agg(2)
+        w2_raw[4] = load_w2(4)
+        w2_raw[6] = load_w2(6)
+        for j in range(3, len(TILES)):
+            x_raw[j] = load_x(j)
+            agg_raw[j] = load_agg(j)
+        hidden(0, (2, 3))
+        a1 = regroup_image(agg_raw[1], True)
+        quantise_image(1, 0, x1)
+        regroup_hidden(0, 0)
+        quantise_image(1, X_PASSES, a1)
+        quantise_hidden(0, 0)
+        transpose_w1(4)
+        transpose_w1(5)
+        quantise_w1(4)
+        quantise_w1(5)
+        hidden(1, low)
+        transpose_w1(6)
+        transpose_w1(7)
+        regroup_hidden(1, 0)
+        x2 = regroup_pass(x_raw[2], 0, "vector")
+        quantise_hidden(1, 0)
+        quantise_w1(6)
+        quantise_w1(7)
+        hidden(0, high)
+        x3 = regroup_pass(x_raw[2], 1, "vector")
+        quantise_pass(2, 0, x2)
+        transpose_w2(0)
+        transpose_w2(2)
+        a3 = regroup_pass(agg_raw[2], 1, "scalar")
+        a2 = regroup_pass(agg_raw[2], 0, "vector")
+        quantise_pass(2, 1, x3)
+        regroup_hidden(0, 1)
+        quantise_pass(2, 2, a2)
+        quantise_hidden(0, 1)
+        hidden(1, high)
+        quantise_pass(2, 3, a3)
+        quantise_w2(0)
+        quantise_w2(2)
+        regroup_hidden(1, 1)
+        transpose_w2(4)
+        transpose_w2(6)
+        quantise_hidden(1, 1)
+        hidden(2, (0, 1))
+        x4 = regroup_image(x_raw[3], False)
+        quantise_w2(4)
+        quantise_w2(6)
+        quantise_image(3, 0, x4)
+        hidden(2, (2, 3))
+        a4 = regroup_image(agg_raw[3], True)
+        regroup_hidden(2, 0)
+        quantise_image(3, X_PASSES, a4)
+        quantise_hidden(2, 0)
+        r0 = gate(0, low)
+        hidden(2, high)
+        x5 = regroup_image(x_raw[4], False)
+        apply_gate(0, low, r0)
+        quantise_image(4, 0, x5)
+        r1 = gate(1, low)
+        a5 = regroup_image(agg_raw[4], True)
+        regroup_hidden(2, 1)
+        quantise_image(4, X_PASSES, a5)
+        quantise_hidden(2, 1)
+        hidden(3, low)
+        apply_gate(1, low, r1)
+        r0 = gate(0, high)
+        regroup_hidden(3, 0)
+        r1 = gate(1, high)
+        apply_gate(0, high, r0)
+        quantise_hidden(3, 0)
+        hidden(3, high)
+        apply_gate(1, high, r1)
+        r0 = gate(2, (0, 1))
+        regroup_hidden(3, 1)
+        apply_gate(2, (0, 1), r0)
+        quantise_hidden(3, 1)
+        hidden(4, (0, 1))
+        r0 = gate(2, (2, 3))
+        hidden(4, (2, 3))
+        apply_gate(2, (2, 3), r0)
+        r0 = gate(2, (4, 5))
+        regroup_hidden(4, 0)
+        r1 = gate(2, (6, 7))
+        apply_gate(2, (4, 5), r0)
+        quantise_hidden(4, 0)
+        hidden(4, high)
+        apply_gate(2, (6, 7), r1)
+        r0 = gate(3, low)
+        regroup_hidden(4, 1)
+        r1 = gate(3, high)
+        quantise_hidden(4, 1)
+        apply_gate(3, low, r0)
+        apply_gate(3, high, r1)
+        for units in (low, (4, 5), (6,), (7,)):
+            r0 = gate(4, units)
+            apply_gate(4, units, r0)

@@ -66,51 +66,64 @@ def tile_graphaugmentation_pb_kernel(tc, x, agg, g1w, g1b, g2w, g2b, out):
         b1 = keep.tile([P, UNITS], BF16, name="b1")
         b2 = keep.tile([P, UNITS], BF16, name="b2")
 
-        def load_rows(raw, rows, images):
-            for n, b in enumerate(images):
-                nc.sync.dma_start(out=raw[:, n].rearrange("p (g t) w -> p g t w", t=PACK), in_=rows[:, b])
-
-        def load_x(j):
-            pool = x_stage if len(TILES[j]) == 1 else keep
-            raw = pool.tile([P, len(TILES[j]), UNITS, PIX], BF16, name="x_raw%d" % len(TILES[j]))
-            load_rows(raw, x_rows, TILES[j])
-            return raw
-
-        def load_agg(j):
-            raw = keep.tile([P, len(TILES[j]), UNITS, PIX], BF16, name="agg_raw%d" % j)
-            load_rows(raw, agg_rows, TILES[j])
-            return raw
-
-        def load_w1(i):
-            raw = w_raw_stage.tile([P, 2 * CH], BF16, name="w_raw")
-            nc.sync.dma_start(out=raw[:], in_=g1w_rows[:, i // PACK, i % PACK])
-            return raw
-
-        def load_w2(i):
-            raw = w_raw_stage.tile([P, 2, HID], BF16, name="w_raw")
-            nc.sync.dma_start(out=raw[:], in_=g2w_rows[:, i // PACK, i % PACK : i % PACK + 2])
-            return raw
-
+        low, high = (0, 1, 2, 3), (4, 5, 6, 7)
         x_raw = {}
         agg_raw = {}
         w1_raw = {}
         w2_raw = {}
-        w1_raw[0] = load_w1(0)
-        x_raw[0] = load_x(0)
-        w1_raw[1] = load_w1(1)
-        agg_raw[0] = load_agg(0)
-        w1_raw[2] = load_w1(2)
-        w1_raw[3] = load_w1(3)
-        for b_bf, b_dram in ((b1, g1b), (b2, g2b)):
+
+        x_pairs = {}
+        agg_pairs = [keep.tile([P, 2, UNITS, PIX], BF16, name="agg_pair%d" % q) for q in range(IMAGES // 2)]
+        for j, images in enumerate(TILES):
+            first = images[0] % 2
+            agg_raw[j] = agg_pairs[images[0] // 2][:, first : first + len(images)]
+
+        def new_x_pair(q):
+            x_pairs[q] = x_stage.tile([P, 2, UNITS, PIX], BF16, name="x_pair")
+            for j, images in enumerate(TILES):
+                if images[0] // 2 == q:
+                    first = images[0] % 2
+                    x_raw[j] = x_pairs[q][:, first : first + len(images)]
+
+        def load_image(pairs, rows, b):
+            nc.sync.dma_start(
+                out=pairs[b // 2][:, b % 2].rearrange("p (g t) w -> p g t w", t=PACK), in_=rows[:, b]
+            )
+
+        def load_x(b):
+            load_image(x_pairs, x_rows, b)
+
+        def load_agg(b):
+            load_image(agg_pairs, agg_rows, b)
+
+        def load_w1(i):
+            w1_raw[i] = w_raw_stage.tile([P, 2 * CH], BF16, name="w_raw")
+            nc.sync.dma_start(out=w1_raw[i][:], in_=g1w_rows[:, i // PACK, i % PACK])
+
+        def load_w2(i):
+            w2_raw[i] = w_raw_stage.tile([P, 2, HID], BF16, name="w_raw")
+            nc.sync.dma_start(out=w2_raw[i][:], in_=g2w_rows[:, i // PACK, i % PACK : i % PACK + 2])
+
+        def load_bias(b_bf, b_dram):
             nc.sync.dma_start(
                 out=b_bf[:].rearrange("p (g t) -> p g t", g=GROUPS),
                 in_=b_dram.rearrange("(g p t) -> p g t", g=GROUPS, p=P, t=PACK),
             )
-        x_raw[1] = load_x(1)
-        agg_raw[1] = load_agg(1)
-        for i in range(4, UNITS):
-            w1_raw[i] = load_w1(i)
 
+        load_w1(0)
+        new_x_pair(0)
+        load_x(0)
+        load_w1(1)
+        load_agg(0)
+        load_w1(2)
+        load_w1(3)
+        load_bias(b1, g1b)
+        load_x(1)
+        load_agg(1)
+        load_w1(4)
+        load_w1(5)
+        load_w1(6)
+        load_w1(7)
         def operand(name, shape):
             codes = keep.tile([P] + shape, U32, name=name + "_codes", align_bytes=64)
             scales = keep.tile([P] + shape, U8, name=name + "_scales", align_bytes=64)
@@ -263,13 +276,12 @@ def tile_graphaugmentation_pb_kernel(tc, x, agg, g1w, g1b, g2w, g2b, out):
                 out=out_rows[:, b0 : b0 + len(TILES[j]), first // PACK, t0 : t0 + len(units)], in_=res[:]
             )
 
-        low, high = (0, 1, 2, 3), (4, 5, 6, 7)
         transpose_w1(0)
         x0 = regroup_image(x_raw[0], False)
         quantise_w1(0)
-        quantise_image(0, 0, x0)
         transpose_w1(1)
         a0 = regroup_image(agg_raw[0], False)
+        quantise_image(0, 0, x0)
         quantise_w1(1)
         quantise_image(0, X_PASSES, a0)
         transpose_w1(2)
@@ -278,102 +290,109 @@ def tile_graphaugmentation_pb_kernel(tc, x, agg, g1w, g1b, g2w, g2b, out):
         quantise_w1(2)
         quantise_w1(3)
         x1 = regroup_image(x_raw[1], False)
-        x_raw[2] = load_x(2)
-        w2_raw[0] = load_w2(0)
-        w2_raw[2] = load_w2(2)
-        agg_raw[2] = load_agg(2)
-        w2_raw[4] = load_w2(4)
-        w2_raw[6] = load_w2(6)
-        for j in range(3, len(TILES)):
-            x_raw[j] = load_x(j)
-            agg_raw[j] = load_agg(j)
+        new_x_pair(1)
+        for b in (2, 3):
+            load_x(b)
+        load_w2(0)
+        load_w2(2)
+        for b in (2, 3):
+            load_agg(b)
+        load_bias(b2, g2b)
+        load_w2(4)
+        load_w2(6)
+        new_x_pair(2)
+        for b in (4, 5):
+            load_x(b)
+            load_agg(b)
         hidden(0, (2, 3))
         a1 = regroup_image(agg_raw[1], True)
         quantise_image(1, 0, x1)
-        regroup_hidden(0, 0)
-        quantise_image(1, X_PASSES, a1)
-        quantise_hidden(0, 0)
         transpose_w1(4)
         transpose_w1(5)
+        regroup_hidden(0, 0)
+        quantise_image(1, X_PASSES, a1)
         quantise_w1(4)
         quantise_w1(5)
+        quantise_hidden(0, 0)
         hidden(1, low)
         transpose_w1(6)
         transpose_w1(7)
         regroup_hidden(1, 0)
-        x2 = regroup_pass(x_raw[2], 0, "vector")
-        quantise_hidden(1, 0)
+        hidden(0, (4, 5))
         quantise_w1(6)
         quantise_w1(7)
-        hidden(0, high)
+        quantise_hidden(1, 0)
+        x2 = regroup_pass(x_raw[2], 0, "vector")
+        hidden(0, (6, 7))
         x3 = regroup_pass(x_raw[2], 1, "vector")
-        quantise_pass(2, 0, x2)
         transpose_w2(0)
         transpose_w2(2)
-        a3 = regroup_pass(agg_raw[2], 1, "scalar")
-        a2 = regroup_pass(agg_raw[2], 0, "vector")
-        quantise_pass(2, 1, x3)
+        quantise_pass(2, 0, x2)
         regroup_hidden(0, 1)
-        quantise_pass(2, 2, a2)
+        quantise_pass(2, 1, x3)
+        a2 = regroup_pass(agg_raw[2], 0, "vector")
+        hidden(1, (4, 5))
+        a3 = regroup_pass(agg_raw[2], 1, "scalar")
         quantise_hidden(0, 1)
-        hidden(1, high)
-        quantise_pass(2, 3, a3)
-        quantise_w2(0)
-        quantise_w2(2)
-        regroup_hidden(1, 1)
+        quantise_pass(2, 2, a2)
+        hidden(1, (6, 7))
         transpose_w2(4)
         transpose_w2(6)
-        quantise_hidden(1, 1)
+        quantise_pass(2, 3, a3)
         hidden(2, (0, 1))
+        regroup_hidden(1, 1)
+        quantise_w2(0)
+        quantise_w2(2)
+        quantise_hidden(1, 1)
         x4 = regroup_image(x_raw[3], False)
+        a4 = regroup_image(agg_raw[3], True)
+        hidden(2, (2, 3))
+        r0 = gate(0, low)
+        quantise_image(3, 0, x4)
+        x5 = regroup_image(x_raw[4], False)
+        quantise_image(3, X_PASSES, a4)
+        a5 = regroup_image(agg_raw[4], True)
         quantise_w2(4)
         quantise_w2(6)
-        quantise_image(3, 0, x4)
-        hidden(2, (2, 3))
-        a4 = regroup_image(agg_raw[3], True)
-        regroup_hidden(2, 0)
-        quantise_image(3, X_PASSES, a4)
-        quantise_hidden(2, 0)
-        r0 = gate(0, low)
         hidden(2, high)
-        x5 = regroup_image(x_raw[4], False)
-        apply_gate(0, low, r0)
         quantise_image(4, 0, x5)
         r1 = gate(1, low)
-        a5 = regroup_image(agg_raw[4], True)
-        regroup_hidden(2, 1)
+        apply_gate(0, low, r0)
         quantise_image(4, X_PASSES, a5)
-        quantise_hidden(2, 1)
+        regroup_hidden(2, 0)
         hidden(3, low)
-        apply_gate(1, low, r1)
         r0 = gate(0, high)
-        regroup_hidden(3, 0)
+        quantise_hidden(2, 0)
+        apply_gate(1, low, r1)
         r1 = gate(1, high)
-        apply_gate(0, high, r0)
+        regroup_hidden(2, 1)
+        regroup_hidden(3, 0)
+        quantise_hidden(2, 1)
         quantise_hidden(3, 0)
         hidden(3, high)
-        apply_gate(1, high, r1)
+        apply_gate(0, high, r0)
         r0 = gate(2, (0, 1))
+        apply_gate(1, high, r1)
+        hidden(4, (0, 1))
         regroup_hidden(3, 1)
+        r1 = gate(2, (2, 3))
         apply_gate(2, (0, 1), r0)
         quantise_hidden(3, 1)
-        hidden(4, (0, 1))
-        r0 = gate(2, (2, 3))
         hidden(4, (2, 3))
-        apply_gate(2, (2, 3), r0)
         r0 = gate(2, (4, 5))
-        regroup_hidden(4, 0)
+        apply_gate(2, (2, 3), r1)
         r1 = gate(2, (6, 7))
+        regroup_hidden(4, 0)
         apply_gate(2, (4, 5), r0)
         quantise_hidden(4, 0)
-        hidden(4, high)
-        apply_gate(2, (6, 7), r1)
         r0 = gate(3, low)
+        apply_gate(2, (6, 7), r1)
+        hidden(4, high)
+        apply_gate(3, low, r0)
         regroup_hidden(4, 1)
         r1 = gate(3, high)
         quantise_hidden(4, 1)
-        apply_gate(3, low, r0)
         apply_gate(3, high, r1)
-        for units in (low, (4, 5), (6,), (7,)):
+        for units in ((0, 1), (2, 3), (4, 5), (6,), (7,)):
             r0 = gate(4, units)
             apply_gate(4, units, r0)

@@ -50,7 +50,7 @@ def tile_graphaugmentation_pb_kernel(tc, x, agg, g1w, g1b, g2w, g2b, out):
         w_stage = ctx.enter_context(tc.tile_pool(name="w_stage", bufs=4))
         w_raw_stage = ctx.enter_context(tc.tile_pool(name="w_raw_stage", bufs=UNITS))
         hid_stage = ctx.enter_context(tc.tile_pool(name="hid_stage", bufs=2))
-        res_stage = ctx.enter_context(tc.tile_pool(name="res_stage", bufs=8))
+        res_stage = ctx.enter_context(tc.tile_pool(name="res_stage", bufs=6))
         x_stage = ctx.enter_context(tc.tile_pool(name="x_stage", bufs=2))
         psum = ctx.enter_context(tc.psum_pool(name="psum", bufs=PSUM_BANKS))
         ctx.enter_context(tc.manual_schedule())
@@ -125,8 +125,8 @@ def tile_graphaugmentation_pb_kernel(tc, x, agg, g1w, g1b, g2w, g2b, out):
         load_w1(6)
         load_w1(7)
         def operand(name, shape):
-            codes = keep.tile([P] + shape, U32, name=name + "_codes", align_bytes=64)
-            scales = keep.tile([P] + shape, U8, name=name + "_scales", align_bytes=64)
+            codes = keep.tile([P] + shape, U32, name=name + "_codes", align_bytes=256)
+            scales = keep.tile([P] + shape, U8, name=name + "_scales", align_bytes=256)
             return codes, scales
 
         cat_mx = [operand("cat%d" % j, [C_PASSES, PIX * len(TILES[j])]) for j in range(len(TILES))]

from contextlib import ExitStack

import concourse.mybir as mybir
from concourse.masks import make_identity

F32 = mybir.dt.float32
BF16 = mybir.dt.bfloat16
U32 = mybir.dt.uint32
U8 = mybir.dt.uint8
FP8X4 = mybir.dt.float8_e4m3fn_x4
ACT = mybir.ActivationFunctionType
ALU = mybir.AluOpType

P = 128
PACK = 4
GROUPS = 2
UNITS = GROUPS * PACK
HALVES = 2
IMAGES = 6
CH = 1024
PIX = 256
HID = 1024
C_PASSES = 2 * CH // (P * PACK)
X_PASSES = C_PASSES // 2
G_PASSES = HID // (P * PACK)
BANK_PASSES = 2
PSUM_BANKS = 8
RUN = 4

TILES = ((0,), (1,), (2, 3), (4,), (5,))

FLOPS = 2 * IMAGES * PIX * (2 * CH * HID + HID * CH)


def tile_graphaugmentation_pb_kernel(tc, x, agg, g1w, g1b, g2w, g2b, out):
    nc = tc.nc

    def by_units(images):
        return images.rearrange("b (g p t) h w -> p b g t (h w)", g=GROUPS, p=P, t=PACK)

    x_rows = by_units(x)
    agg_rows = by_units(agg)
    out_rows = by_units(out)
    g1w_rows = g1w.rearrange("(g p t) c -> p g t c", g=GROUPS, p=P, t=PACK)
    g2w_rows = g2w.rearrange("(g p t) k -> p g t k", g=GROUPS, p=P, t=PACK)

    with ExitStack() as ctx:
        keep = ctx.enter_context(tc.tile_pool(name="keep", bufs=1))
        cat_stage = ctx.enter_context(tc.tile_pool(name="cat_stage", bufs=4))
        w_stage = ctx.enter_context(tc.tile_pool(name="w_stage", bufs=4))
        w_raw_stage = ctx.enter_context(tc.tile_pool(name="w_raw_stage", bufs=UNITS))
        hid_stage = ctx.enter_context(tc.tile_pool(name="hid_stage", bufs=2))
        res_stage = ctx.enter_context(tc.tile_pool(name="res_stage", bufs=6))
        x_stage = ctx.enter_context(tc.tile_pool(name="x_stage", bufs=2))
        psum = ctx.enter_context(tc.psum_pool(name="psum", bufs=PSUM_BANKS))
        ctx.enter_context(tc.manual_schedule())

        ident = keep.tile([P, P], F32, name="ident")
        make_identity(nc, ident[:])

        zero = keep.tile([P, 1], F32, name="zero")
        half = keep.tile([P, 1], F32, name="half")
        nc.vector.memset(zero[:], 0.0)
        nc.scalar.activation(out=half[:], in_=zero[:], func=ACT.Sigmoid)

        b1 = keep.tile([P, UNITS], BF16, name="b1")
        b2 = keep.tile([P, UNITS], BF16, name="b2")

        low, high = (0, 1, 2, 3), (4, 5, 6, 7)
        x_raw = {}
        agg_raw = {}
        w1_raw = {}
        w2_raw = {}

        x_pairs = {}
        agg_pairs = [keep.tile([P, 2, UNITS, PIX], BF16, name="agg_pair%d" % q) for q in range(IMAGES // 2)]
        for j, images in enumerate(TILES):
            first = images[0] % 2
            agg_raw[j] = agg_pairs[images[0] // 2][:, first : first + len(images)]

        def new_x_pair(q):
            x_pairs[q] = x_stage.tile([P, 2, UNITS, PIX], BF16, name="x_pair")
            for j, images in enumerate(TILES):
                if images[0] // 2 == q:
                    first = images[0] % 2
                    x_raw[j] = x_pairs[q][:, first : first + len(images)]

        def load_image(pairs, rows, b):
            nc.sync.dma_start(
                out=pairs[b // 2][:, b % 2].rearrange("p (g t) w -> p g t w", t=PACK), in_=rows[:, b]
            )

        def load_x(b):
            load_image(x_pairs, x_rows, b)

        def load_agg(b):
            load_image(agg_pairs, agg_rows, b)

        def load_w1(i):
            w1_raw[i] = w_raw_stage.tile([P, 2 * CH], BF16, name="w_raw")
            nc.sync.dma_start(out=w1_raw[i][:], in_=g1w_rows[:, i // PACK, i % PACK])

        def load_w2(i):
            w2_raw[i] = w_raw_stage.tile([P, 2, HID], BF16, name="w_raw")
            nc.sync.dma_start(out=w2_raw[i][:], in_=g2w_rows[:, i // PACK, i % PACK : i % PACK + 2])

        def load_bias(b_bf, b_dram):
            nc.sync.dma_start(
                out=b_bf[:].rearrange("p (g t) -> p g t", g=GROUPS),
                in_=b_dram.rearrange("(g p t) -> p g t", g=GROUPS, p=P, t=PACK),
            )

        load_w1(0)
        new_x_pair(0)
        load_x(0)
        load_w1(1)
        load_agg(0)
        load_w1(2)
        load_w1(3)
        load_bias(b1, g1b)
        load_x(1)
        load_agg(1)
        load_w1(4)
        load_w1(5)
        load_w1(6)
        load_w1(7)
        def operand(name, shape):
            codes = keep.tile([P] + shape, U32, name=name + "_codes", align_bytes=256)
            scales = keep.tile([P] + shape, U8, name=name + "_scales", align_bytes=256)
            return codes, scales

        cat_mx = [operand("cat%d" % j, [C_PASSES, PIX * len(TILES[j])]) for j in range(len(TILES))]
        hid_mx = [operand("hid%d" % j, [G_PASSES, PIX * len(TILES[j])]) for j in range(len(TILES))]
        w1_mx = [operand("w1_%d" % i, [C_PASSES, P]) for i in range(UNITS)]
        w2_mx = [operand("w2_%d" % i, [2, G_PASSES, P]) for i in range(0, UNITS, 2)]

        def quantise(mx, where, grouped):
            codes, scales = mx
            nc.vector.quantize_mx(
                out=codes[:, where].rearrange("p a n -> p (a n)").bitcast(FP8X4),
                scales=scales[:, where].rearrange("p a n -> p (a n)"),
                in_=grouped,
            )

        def regroup_image(raw, shared):
            grouped = cat_stage.tile([P, X_PASSES, PIX, PACK], BF16, name="cat_grouped", align_bytes=64)
            dst = grouped[:].rearrange("p g (c i) t -> p g c t i", i=RUN)
            src = raw[:, 0].rearrange("p (g t) (c i) -> p g c t i", t=PACK, i=RUN)
            if shared:
                nc.vector.tensor_copy(out=dst[:, 0], in_=src[:, 0])
                nc.scalar.copy(out=dst[:, 1], in_=src[:, 1])
            else:
                nc.vector.tensor_copy(out=dst, in_=src)
            return grouped

        def quantise_image(j, first, grouped):
            quantise(cat_mx[j], slice(first, first + X_PASSES), grouped[:].rearrange("p g n t -> p (g n t)"))

        def regroup_pass(raw, g, engine_copy):
            grouped = cat_stage.tile([P, 2, PIX, PACK], BF16, name="cat_grouped", align_bytes=64)
            dst = grouped[:].rearrange("p b (c i) t -> p b c t i", i=RUN)
            src = raw[:, :, PACK * g : PACK * g + PACK, :].rearrange("p b t (c i) -> p b c t i", i=RUN)
            if engine_copy == "scalar":
                for b in range(2):
                    nc.scalar.copy(out=dst[:, b], in_=src[:, b])
            else:
                nc.vector.tensor_copy(out=dst, in_=src)
            return grouped

        def quantise_pass(j, G, grouped):
            quantise(cat_mx[j], slice(G, G + 1), grouped[:].rearrange("p b n t -> p (b n t)"))

        def transpose_rows(words, passes, grouped_words):
            for G0 in range(0, passes, BANK_PASSES):
                bank = psum.tile([P, BANK_PASSES, HALVES, P], F32, name="t_bank", tag="bank")
                for G in range(G0, G0 + BANK_PASSES):
                    for u in range(HALVES):
                        first = P * HALVES * G
                        nc.tensor.transpose(
                            out=bank[:, G - G0, u, :],
                            in_=words[:, first + u : first + P * HALVES : HALVES],
                            identity=ident[:],
                        )
                nc.scalar.copy(
                    out=grouped_words[:, G0 : G0 + BANK_PASSES, :, :],
                    in_=bank[:].rearrange("p g u m -> p g m u"),
                )

        w_grouped = {}

        def transpose_w1(i):
            w_grouped[i] = w_stage.tile([P, C_PASSES, P, PACK], BF16, name="w_grouped", align_bytes=64)
            transpose_rows(w1_raw[i][:].bitcast(F32), C_PASSES, w_grouped[i][:].bitcast(F32))

        def quantise_w1(i):
            quantise(w1_mx[i], slice(0, C_PASSES), w_grouped[i][:].rearrange("p g m t -> p (g m t)"))

        def transpose_w2(i):
            w_grouped[i] = w_stage.tile([P, 2, G_PASSES, P, PACK], BF16, name="w_grouped", align_bytes=64)
            for e in range(2):
                transpose_rows(w2_raw[i][:].bitcast(F32)[:, e], G_PASSES, w_grouped[i][:].bitcast(F32)[:, e])

        def quantise_w2(i):
            codes, scales = w2_mx[i // 2]
            nc.vector.quantize_mx(
                out=codes[:].rearrange("p e g m -> p (e g m)").bitcast(FP8X4),
                scales=scales[:].rearrange("p e g m -> p (e g m)"),
                in_=w_grouped[i][:].rearrange("p e g m t -> p (e g m t)"),
            )

        def product(codes, scales, passes, rhs):
            rhs_codes, rhs_scales = rhs
            acc = psum.tile([P, rhs_codes.shape[2]], F32, name="acc", tag="bank")
            for G in range(passes):
                nc.tensor.matmul_mx(
                    out=acc[:],
                    lhsT=codes[:, G, :].bitcast(FP8X4),
                    lhsT_scale=scales[:, G, :],
                    rhs=rhs_codes[:, G, :].bitcast(FP8X4),
                    rhs_scale=rhs_scales[:, G, :],
                    start=(G == 0),
                    stop=(G == passes - 1),
                )
            return acc

        hid = {}

        def hidden(j, units):
            for i in units:
                G = i // PACK
                if i % PACK == 0:
                    hid[j, G] = hid_stage.tile([P, PACK, PIX * len(TILES[j])], BF16, name="hid%d" % len(TILES[j]))
                acc = product(w1_mx[i][0], w1_mx[i][1], C_PASSES, cat_mx[j])
                nc.scalar.activation(
                    out=hid[j, G][:, i % PACK, :], in_=acc[:], func=ACT.Relu, bias=b1[:, i : i + 1], scale=1.0
                )

        hid_grouped = {}

        def regroup_hidden(j, G):
            columns = PIX * len(TILES[j])
            hid_grouped[j, G] = hid_stage.tile(
                [P, columns, PACK], BF16, name="hid_grouped%d" % len(TILES[j]), align_bytes=64
            )
            nc.vector.tensor_copy(
                out=hid_grouped[j, G][:].rearrange("p (c i) t -> p c t i", i=RUN),
                in_=hid[j, G][:].rearrange("p t (c i) -> p c t i", i=RUN),
            )

        def quantise_hidden(j, G):
            quantise(hid_mx[j], slice(G, G + 1), hid_grouped[j, G][:].rearrange("p n t -> p (n t)"))

        def gate(j, units):
            images = len(TILES[j])
            res = res_stage.tile([P, images, len(units), PIX], F32, name="res")
            for n, i in enumerate(units):
                codes, scales = w2_mx[i // 2]
                acc = product(codes[:, i % 2], scales[:, i % 2], G_PASSES, hid_mx[j])
                nc.scalar.activation(
                    out=res[:, :, n, :],
                    in_=acc[:].rearrange("p (b w) -> p b w", b=images),
                    func=ACT.Sigmoid,
                    bias=b2[:, i : i + 1],
                    scale=1.0,
                )
            return res

        def apply_gate(j, units, res):
            first, last = units[0], units[-1]
            nc.vector.tensor_tensor(
                out=res[:], in0=res[:], in1=agg_raw[j][:, :, first : last + 1, :], op=ALU.mult
            )
            b0 = TILES[j][0]
            t0 = first % PACK
            nc.sync.dma_start(
                out=out_rows[:, b0 : b0 + len(TILES[j]), first // PACK, t0 : t0 + len(units)], in_=res[:]
            )

        transpose_w1(0)
        x0 = regroup_image(x_raw[0], False)
        quantise_w1(0)
        transpose_w1(1)
        a0 = regroup_image(agg_raw[0], False)
        quantise_image(0, 0, x0)
        quantise_w1(1)
        quantise_image(0, X_PASSES, a0)
        transpose_w1(2)
        transpose_w1(3)
        hidden(0, (0, 1))
        quantise_w1(2)
        quantise_w1(3)
        x1 = regroup_image(x_raw[1], False)
        new_x_pair(1)
        for b in (2, 3):
            load_x(b)
        load_w2(0)
        load_w2(2)
        for b in (2, 3):
            load_agg(b)
        load_bias(b2, g2b)
        load_w2(4)
        load_w2(6)
        new_x_pair(2)
        for b in (4, 5):
            load_x(b)
            load_agg(b)
        hidden(0, (2, 3))
        a1 = regroup_image(agg_raw[1], True)
        quantise_image(1, 0, x1)
        transpose_w1(4)
        transpose_w1(5)
        regroup_hidden(0, 0)
        quantise_image(1, X_PASSES, a1)
        quantise_w1(4)
        quantise_w1(5)
        quantise_hidden(0, 0)
        hidden(1, low)
        transpose_w1(6)
        transpose_w1(7)
        regroup_hidden(1, 0)
        hidden(0, (4, 5))
        quantise_w1(6)
        quantise_w1(7)
        quantise_hidden(1, 0)
        x2 = regroup_pass(x_raw[2], 0, "vector")
        hidden(0, (6, 7))
        x3 = regroup_pass(x_raw[2], 1, "vector")
        transpose_w2(0)
        transpose_w2(2)
        quantise_pass(2, 0, x2)
        regroup_hidden(0, 1)
        quantise_pass(2, 1, x3)
        a2 = regroup_pass(agg_raw[2], 0, "vector")
        hidden(1, (4, 5))
        a3 = regroup_pass(agg_raw[2], 1, "scalar")
        quantise_hidden(0, 1)
        quantise_pass(2, 2, a2)
        hidden(1, (6, 7))
        transpose_w2(4)
        transpose_w2(6)
        quantise_pass(2, 3, a3)
        hidden(2, (0, 1))
        regroup_hidden(1, 1)
        quantise_w2(0)
        quantise_w2(2)
        quantise_hidden(1, 1)
        x4 = regroup_image(x_raw[3], False)
        a4 = regroup_image(agg_raw[3], True)
        hidden(2, (2, 3))
        r0 = gate(0, low)
        quantise_image(3, 0, x4)
        x5 = regroup_image(x_raw[4], False)
        quantise_image(3, X_PASSES, a4)
        a5 = regroup_image(agg_raw[4], True)
        quantise_w2(4)
        quantise_w2(6)
        hidden(2, high)
        quantise_image(4, 0, x5)
        r1 = gate(1, low)
        apply_gate(0, low, r0)
        quantise_image(4, X_PASSES, a5)
        regroup_hidden(2, 0)
        hidden(3, low)
        r0 = gate(0, high)
        quantise_hidden(2, 0)
        apply_gate(1, low, r1)
        r1 = gate(1, high)
        regroup_hidden(2, 1)
        regroup_hidden(3, 0)
        quantise_hidden(2, 1)
        quantise_hidden(3, 0)
        hidden(3, high)
        apply_gate(0, high, r0)
        r0 = gate(2, (0, 1))
        apply_gate(1, high, r1)
        hidden(4, (0, 1))
        regroup_hidden(3, 1)
        r1 = gate(2, (2, 3))
        apply_gate(2, (0, 1), r0)
        quantise_hidden(3, 1)
        hidden(4, (2, 3))
        r0 = gate(2, (4, 5))
        apply_gate(2, (2, 3), r1)
        r1 = gate(2, (6, 7))
        regroup_hidden(4, 0)
        apply_gate(2, (4, 5), r0)
        quantise_hidden(4, 0)
        r0 = gate(3, low)
        apply_gate(2, (6, 7), r1)
        hidden(4, high)
        apply_gate(3, low, r0)
        regroup_hidden(4, 1)
        r1 = gate(3, high)
        quantise_hidden(4, 1)
        apply_gate(3, high, r1)
        for units in ((0, 1), (2, 3), (4, 5), (6,), (7,)):
            r0 = gate(4, units)
            apply_gate(4, units, r0)
